import numpy as np
import ml_dtypes


def mxq(x, axis, fmt="e4m3"):
    dtype, down = {"e4m3": (ml_dtypes.float8_e4m3fn, 7), "e5m2": (ml_dtypes.float8_e5m2, 14)}[fmt]
    v = np.moveaxis(np.asarray(x, np.float32).astype(ml_dtypes.bfloat16).astype(np.float64), axis, -1)
    blocks = v.reshape(v.shape[:-1] + (-1, 32))
    amax = np.abs(blocks).max(-1, keepdims=True)
    byte = np.maximum(np.where(amax > 0, np.frexp(amax)[1] - 1 + 127, 0) - down, 1)
    scale = np.exp2(byte - 127.0)
    codes = (blocks / scale).astype(np.float32).astype(dtype).astype(np.float64)
    return np.moveaxis((codes * scale).reshape(v.shape), -1, axis)


WIDE = False


def mx_kscale(k):
    if not WIDE:
        return np.ones(k)
    levels = np.array([10, -10, 5, -5, 0])
    if k % 512:
        return np.exp2(np.random.permutation(np.resize(levels, k // 32))).repeat(32)
    a = np.empty((k // 512, 16))
    for p in range(k // 512):
        a[p, :8] = np.random.permutation(np.resize(levels, 8))
        for g in range(8):
            far = levels[np.abs(levels - a[p, g]) >= 10]
            a[p, g + 8] = far[np.random.randint(len(far))]
    return np.exp2(a.ravel()).repeat(32)


BF16 = ml_dtypes.bfloat16


def bf(x):
    return np.asarray(x, np.float32).astype(BF16)


def f64(x):
    return np.asarray(x).astype(np.float64)


B, I, H = 512, 1024, 1024
EPS = 1e-12
FORGET_BIAS = 1.0


def layer_norm(x, g, b):
    mean = np.mean(x, axis=-1, keepdims=True)
    var = np.mean((x - mean) ** 2, axis=-1, keepdims=True)
    var_filter = 0.01 * (var < EPS).astype(np.float64)
    normalized = (x - mean) / np.sqrt(var + EPS + var_filter)
    return g * normalized + b


def sigmoid(v):
    return 1.0 / (1.0 + np.exp(-v))


def draw0():
    s, t = mx_kscale(I), mx_kscale(H)
    return {"x": bf(np.random.standard_normal((B, I)) * s),
            "hx": bf(np.random.standard_normal((B, H)) * t),
            "cx": bf(np.random.standard_normal((B, H))),
            "weight_ih": bf(np.random.standard_normal((4 * H, I)) / np.sqrt(I) / s[None, :]),
            "weight_hh": bf(np.random.standard_normal((4 * H, H)) / np.sqrt(H) / t[None, :]),
            "gamma": bf(1.0 + 0.1 * np.random.standard_normal((5, H))),
            "beta": bf(0.1 * np.random.standard_normal((5, H)))}


def core(x, hx, cx, weight_ih, weight_hh, gamma, beta):
    cx, gamma, beta = f64(cx), f64(gamma), f64(beta)
    gates = (mxq(f64(x), 1, "e4m3") @ mxq(f64(weight_ih), 1, "e4m3").T) + (mxq(f64(hx), 1, "e4m3") @ mxq(f64(weight_hh), 1, "e4m3").T)
    ingate, forgetgate, cellgate, outgate = np.split(gates, 4, axis=1)
    ingate = layer_norm(ingate, gamma[0], beta[0])
    forgetgate = layer_norm(forgetgate, gamma[1], beta[1])
    cellgate = layer_norm(cellgate, gamma[2], beta[2])
    outgate = layer_norm(outgate, gamma[3], beta[3])
    ingate = sigmoid(ingate)
    forgetgate = sigmoid(forgetgate + FORGET_BIAS)
    cellgate = np.tanh(cellgate)
    outgate = sigmoid(outgate)
    cy = forgetgate * cx + ingate * cellgate
    cy = layer_norm(cy, gamma[4], beta[4])
    hy = outgate * np.tanh(cy)
    hy_dropped = hy
    return (hy_dropped, hy, cy)


def e4m3fn_bytes(y):
    return np.clip(np.asarray(y, np.float64), -448.0, 448.0).astype(np.float32).astype(ml_dtypes.float8_e4m3fn).view(np.uint8)


def e4m3fn_values(b):
    return np.asarray(b, np.uint8).view(ml_dtypes.float8_e4m3fn).astype(np.float64)


def setup_inputs():
    d = draw0()
    x0 = np.asarray(d['weight_ih']).astype(np.float64)
    s = (np.max(np.abs(x0), axis=(0,), keepdims=True) / 448.0).astype(np.float32)
    out = {}
    for k, v in d.items():
        if k == 'weight_ih':
            out['weight_ih_bytes'] = e4m3fn_bytes(x0 / s.astype(np.float64))
            out['weight_ih_scale'] = s
        else:
            out[k] = v
    return out


def reference(x, hx, cx, weight_ih_bytes, weight_ih_scale, weight_hh, gamma, beta):
    return core(x, hx, cx, e4m3fn_values(weight_ih_bytes) * weight_ih_scale.astype(np.float64), weight_hh, gamma, beta)

@@ -1,0 +1,476 @@
+from contextlib import ExitStack
+
+import concourse.mybir as mybir
+from concourse.masks import make_identity
+
+F32 = mybir.dt.float32
+BF16 = mybir.dt.bfloat16
+U32 = mybir.dt.uint32
+U8 = mybir.dt.uint8
+FP8 = mybir.dt.float8_e4m3fn
+FP8X4 = mybir.dt.float8_e4m3fn_x4
+ALU = mybir.AluOpType
+ACT = mybir.ActivationFunctionType
+
+B, I, H = 512, 1024, 1024
+EPS = 1e-12
+P = 128
+MT = B // P
+JT = H // P
+FLOPS = 2 * B * 4 * H * (I + H)
+
+X_UNIT, HX_UNIT = -2, -1
+SEQ = [-2, -1, 1, 0, 2, 3, 5, 4, 6, 7, 9, 8, 10, 11, 13, 12, 14, 15]
+FIRST = -6
+TURN_AT = dict((FIRST + i, w) for i, w in enumerate(SEQ))
+STEP_OF = dict((w, s) for s, w in TURN_AT.items())
+LOADS = {
+    -6: [1, -2, "gb", -1, 3, 0, 2, 5],
+    -5: [4],
+    -4: [6, 7],
+    -2: ["cx", 9],
+    -1: [8],
+    0: [11],
+    2: [10, 13],
+    3: [12],
+    4: [15],
+    6: [14, "g4"],
+}
+
+
+def tile_layernormdropoutlstmcell_kernel(
+    tc, x, hx, cx, wih_bytes, wih_scale, whh, gamma, beta, out_0, out_1, out_2
+):
+    nc = tc.nc
+    with ExitStack() as ctx:
+        const = ctx.enter_context(tc.tile_pool(name="const", bufs=1))
+        stage = ctx.enter_context(tc.tile_pool(name="stage", bufs=4))
+        bytes_pool = ctx.enter_context(tc.tile_pool(name="bytesp", bufs=3))
+        wide = ctx.enter_context(tc.tile_pool(name="wide", bufs=8))
+        grp = ctx.enter_context(tc.tile_pool(name="grp", bufs=2))
+        keep = ctx.enter_context(tc.tile_pool(name="keep", bufs=1))
+        wq = ctx.enter_context(tc.tile_pool(name="wq", bufs=2))
+        nrm = ctx.enter_context(tc.tile_pool(name="nrm", bufs=6))
+        gates = ctx.enter_context(tc.tile_pool(name="gates", bufs=3))
+        work = ctx.enter_context(tc.tile_pool(name="work", bufs=4))
+        small = ctx.enter_context(tc.tile_pool(name="small", bufs=8))
+        ps_bank = ctx.enter_context(tc.psum_pool(name="ps_bank", bufs=3))
+        ps_acc = ctx.enter_context(tc.psum_pool(name="ps_acc", bufs=5))
+
+        ident = const.tile([P, P], F32, name="ident")
+        make_identity(nc, ident[:])
+        ident_bf = const.tile([P, P], BF16, name="ident_bf")
+        make_identity(nc, ident_bf[:])
+
+        ctx.enter_context(tc.manual_schedule())
+
+        neg_half = const.tile([P, 1], F32, name="neg_half")
+        nc.vector.memset(neg_half[:], -0.5)
+        zero_col = const.tile([P, 1], F32, name="zero_col")
+        nc.vector.memset(zero_col[:], 0.0)
+        gb_raw = const.tile([P, P], BF16, name="gb_raw")
+        nc.vector.memset(gb_raw[:], 0.0)
+        warm = const.tile([P, 1], F32, name="warm")
+
+        sc_b = const.tile([P, I], F32, name="sc_b")
+        nc.scalar.dma_start(out=sc_b[:], in_=wih_scale.rearrange("o k -> (o k)").partition_broadcast(P))
+        nc.scalar.activation(out=warm[:], in_=zero_col[:], func=ACT.Sigmoid)
+
+        gam4 = const.tile([P, H], BF16, name="gam4")
+        bet4 = const.tile([P, H], BF16, name="bet4")
+        gb_col = const.tile([P, P], F32, name="gb_col")
+        cxT = const.tile([P, JT, B], BF16, name="cxT")
+
+        src = {}
+        views = {}
+        grouped_of = {}
+        codes = {}
+
+        def w_rows(w):
+            r0 = (w // 4) * H + ((w % 4) // 2) * 512
+            return slice(r0, r0 + 512)
+
+        def load(w):
+            if w == "gb":
+                nc.sync.dma_start(out=gb_raw[0:40, :], in_=gamma.rearrange("a (j c) -> (a j) c", c=P))
+                nc.sync.dma_start(out=gb_raw[40:80, :], in_=beta.rearrange("a (j c) -> (a j) c", c=P))
+            elif w == "g4":
+                nc.sync.dma_start(out=gam4[:], in_=gamma[4:5, :].rearrange("a h -> (a h)").partition_broadcast(P))
+                nc.sync.dma_start(out=bet4[:], in_=beta[4:5, :].rearrange("a h -> (a h)").partition_broadcast(P))
+            elif w == "cx" or w < 0 or w % 2 == 0:
+                raw = stage.tile([P, 4, 1024], BF16, name="raw", tag="raw")
+                rows = cx if w == "cx" else (x if w == X_UNIT else (hx if w == HX_UNIT else whh[w_rows(w), :]))
+                if w != "cx" and w < 0:
+                    for a in range(4):
+                        nc.sync.dma_start(out=raw[:, a, :], in_=rows[a * P : (a + 1) * P, :])
+                else:
+                    nc.sync.dma_start(out=raw[:], in_=rows.rearrange("(a p) k -> p a k", p=P))
+                src[w] = raw
+                if w != "cx":
+                    words = raw[:].bitcast(F32)
+                    views[w] = [words[:, a, :] for a in range(4)]
+            else:
+                wb = bytes_pool.tile([P, 4, 1024], U8, name="wb", tag="wb")
+                nc.sync.dma_start(out=wb[:], in_=wih_bytes[w_rows(w), :].rearrange("(a p) k -> p a k", p=P))
+                src[w] = wb
+                views[w] = []
+
+        def widen_list(s):
+            todo = []
+            for w in (1, 3, 5, 7, 9, 11, 13, 15):
+                d = STEP_OF[w] - s - (1 if w % 4 == 3 else 0)
+                if d == 2:
+                    todo = todo + [(w, 0), (w, 1)]
+                if d == 1:
+                    todo = todo + [(w, 2), (w, 3)]
+            return todo
+
+        def widen(s, which):
+            todo = widen_list(s)
+            for w, a in todo if which is None else todo[which : which + 1]:
+                wbf = wide.tile([P, 1024], BF16, name="wbf", tag="wbf")
+                nc.vector.tensor_tensor(out=wbf[:], in0=src[w][:, a, :].bitcast(FP8), in1=sc_b[:], op=ALU.mult)
+                views[w].append(wbf[:].bitcast(F32))
+
+        def turn(s, first):
+            if s not in TURN_AT:
+                return
+            w = TURN_AT[s]
+            if first:
+                g_new = grp.tile([P, 2, 512, 4], BF16, name="grouped", tag="grouped", align_bytes=64)
+                grouped_of[w] = g_new
+            gw = grouped_of[w][:].bitcast(F32)
+            for a in (0, 1, 2) if first else (3,):
+                bank = ps_bank.tile([P, 2, 2, P], F32, name="bank", tag="bank")
+                for g in range(2):
+                    for u in range(2):
+                        nc.tensor.transpose(
+                            bank[:, g, u, :], views[w][a][:, 256 * g + u : 256 * (g + 1) : 2], ident[:]
+                        )
+                nc.scalar.copy(
+                    out=gw[:, :, a * P : (a + 1) * P, :], in_=bank[:].rearrange("p g u r -> p g r u")
+                )
+
+        def quant(s):
+            if s - 1 not in TURN_AT:
+                return
+            w = TURN_AT[s - 1]
+            if w < 0:
+                c = keep.tile([P, 1024], U32, name="ac%d" % (w + 2), align_bytes=64)
+                s = keep.tile([P, 1024], U8, name="as%d" % (w + 2), align_bytes=64)
+            else:
+                c = wq.tile([P, 1024], U32, name="wc%d" % (w % 4), tag="wc%d" % (w % 4), align_bytes=64)
+                s = wq.tile([P, 1024], U8, name="ws%d" % (w % 4), tag="ws%d" % (w % 4), align_bytes=64)
+            nc.vector.quantize_mx(
+                out=c[:].bitcast(FP8X4), scales=s[:], in_=grouped_of[w][:].rearrange("p g n t -> p (g n t)")
+            )
+            codes[w] = (c, s)
+
+        halves_of = {}
+
+        def matmuls(s, passes):
+            if not 0 <= s <= 15:
+                return
+            q, m = s // 4, s % 4
+            for p8 in passes:
+                half, c4 = p8 // 4, p8 % 4
+                if c4 == 0:
+                    acc_new = ps_acc.tile([P, 512], F32, name="acc", tag="acc")
+                    if half == 0:
+                        halves_of[s] = []
+                    halves_of[s].append(acc_new[:])
+                mat, g = 1 - c4 // 2, c4 % 2
+                wc, ws = codes[4 * q + 2 * half + (1 - mat)]
+                ac, asc = codes[X_UNIT + mat]
+                cols = slice(g * 512 + m * P, g * 512 + (m + 1) * P)
+                nc.tensor.matmul_mx(
+                    out=halves_of[s][half],
+                    lhsT=ac[:, cols].bitcast(FP8X4),
+                    lhsT_scale=asc[:, cols],
+                    rhs=wc[:, g * 512 : (g + 1) * 512].bitcast(FP8X4),
+                    rhs_scale=ws[:, g * 512 : (g + 1) * 512],
+                    start=(c4 == 0),
+                    stop=(c4 == 3),
+                )
+
+        st_of = {}
+        mv_of = {}
+        flt_of = {}
+        rstd_of = {}
+        nmr_of = {}
+
+        def ok(k):
+            return k in halves_of
+
+        def bn(k):
+            if ok(k):
+                st = small.tile([P, 2, 6], F32, name="st", tag="st")
+                for h2 in range(2):
+                    nc.vector.bn_stats(out=st[:, h2, :], in_=halves_of[k][h2])
+                st_of[k] = st
+
+        def aggr(k):
+            if ok(k):
+                mv = small.tile([P, 2], F32, name="mv", tag="mv")
+                nc.vector.bn_aggr(out=mv[:], in_=st_of[k][:].rearrange("p a b -> p (a b)"))
+                mv_of[k] = mv
+
+        def flt(k):
+            if ok(k):
+                f = small.tile([P, 1], F32, name="flt", tag="flt")
+                nc.vector.tensor_scalar(
+                    out=f[:], in0=mv_of[k][:, 1:2], scalar1=EPS, scalar2=0.01, op0=ALU.is_lt, op1=ALU.mult
+                )
+                flt_of[k] = f
+
+        def ve_pow(k):
+            if ok(k):
+                ve = small.tile([P, 1], F32, name="ve", tag="ve")
+                nc.vector.scalar_tensor_tensor(
+                    out=ve[:], in0=mv_of[k][:, 1:2], scalar=EPS, in1=flt_of[k][:], op0=ALU.add, op1=ALU.add
+                )
+                rstd = small.tile([P, 1], F32, name="rstd", tag="rstd")
+                nc.gpsimd.tensor_tensor(out=rstd[:], in0=ve[:], in1=neg_half[:], op=ALU.pow)
+                rstd_of[k] = rstd
+
+        def nmr(k):
+            if ok(k):
+                t = small.tile([P, 1], F32, name="nmr", tag="nmr")
+                nc.vector.tensor_scalar(
+                    out=t[:], in0=mv_of[k][:, 0:1], scalar1=rstd_of[k][:], scalar2=-1.0, op0=ALU.mult, op1=ALU.mult
+                )
+                nmr_of[k] = t
+
+        n_tiles = {0: [], 1: [], 2: [], 3: []}
+        a_tiles = {}
+        FUNC = [ACT.Sigmoid, ACT.Sigmoid, ACT.Tanh, ACT.Sigmoid]
+
+        def normalise(s):
+            if ok(s):
+                n_t = nrm.tile([P, H], F32, name="n_t", tag="n")
+                for h2 in range(2):
+                    nc.scalar.activation(
+                        out=n_t[:, h2 * 512 : (h2 + 1) * 512], in_=halves_of[s][h2], func=ACT.Identity,
+                        scale=rstd_of[s][:], bias=nmr_of[s][:],
+                    )
+                n_tiles[s // 4].append(n_t)
+
+        def ep_cx(jp):
+            bank = ps_bank.tile([P, 2, MT, P], BF16, name="cbank", tag="bank")
+            for j2 in range(2):
+                j = 2 * jp + j2
+                for m in range(MT):
+                    nc.tensor.transpose(bank[:, j2, m, :], src["cx"][:, m, j * P : (j + 1) * P], ident_bf[:])
+            nc.scalar.copy(
+                out=cxT[:, 2 * jp : 2 * jp + 2, :].rearrange("p j t -> p (j t)"),
+                in_=bank[:].rearrange("p j m t -> p (j m t)"),
+            )
+
+        def ep(q, pr, jj):
+            bank = ps_bank.tile([P, 2, 2, P], F32, name="ebank", tag="bank")
+            for j2 in range(2):
+                j = 2 * jj + j2
+                for m2 in range(2):
+                    nc.tensor.transpose(bank[:, j2, m2, :], n_tiles[q][2 * pr + m2][:, j * P : (j + 1) * P], ident[:])
+            if q not in a_tiles:
+                a_new = gates.tile([P, JT, B], F32, name="a_t", tag="a")
+                a_tiles[q] = a_new
+            for j2 in range(2):
+                j = 2 * jj + j2
+                nc.scalar.activation(
+                    out=a_tiles[q][:, j, pr * 256 : (pr + 1) * 256],
+                    in_=bank[:, j2, :, :].rearrange("p m t -> p (m t)"), func=FUNC[q],
+                    scale=gb_col[:, q * 8 + j : q * 8 + j + 1],
+                    bias=gb_col[:, 40 + q * 8 + j : 41 + q * 8 + j],
+                )
+
+        def cell(q, pr, jh):
+            js = slice(4 * jh, 4 * jh + 4)
+            ts = slice(pr * 256, (pr + 1) * 256)
+            if q == 1:
+                nc.vector.tensor_tensor(
+                    out=a_tiles[1][:, js, ts], in0=a_tiles[1][:, js, ts], in1=cxT[:, js, ts], op=ALU.mult
+                )
+            if q == 2:
+                nc.vector.tensor_tensor(
+                    out=a_tiles[2][:, js, ts], in0=a_tiles[2][:, js, ts], in1=a_tiles[0][:, js, ts], op=ALU.mult
+                )
+
+        CX_AT = {1: [0], 2: [1], 3: [2, 3]}
+
+        def b_of(s):
+            if 4 <= s <= 15:
+                return ((s - 4) // 4, ((s - 4) % 4) // 2, (s - 4) % 2)
+            return None
+
+        def b_step(s):
+            for j in CX_AT.get(s, []):
+                ep_cx(j)
+            if b_of(s) is not None:
+                q, pr, jh = b_of(s)
+                ep(q, pr, 2 * jh)
+                ep(q, pr, 2 * jh + 1)
+
+        def cell_step(s):
+            if b_of(s) is not None:
+                q, pr, jh = b_of(s)
+                cell(q, pr, jh)
+
+        for s in range(FIRST, 12):
+            for w in LOADS.get(s, []):
+                load(w)
+            if s < -2:
+                widen(s, None)
+            bn(s - 1)
+            nmr(s - 2)
+            quant(s)
+            if -2 <= s < 0:
+                widen(s, None)
+            aggr(s - 1)
+            turn(s, True)
+            normalise(s - 2)
+            matmuls(s, [0, 1, 2, 3])
+            if s >= 0:
+                widen(s, 0)
+            flt(s - 1)
+            turn(s, False)
+            if s >= 0:
+                widen(s, 1)
+            if s == 1:
+                gb_ps = ps_bank.tile([P, P], BF16, name="gb_ps", tag="bank")
+                nc.tensor.transpose(gb_ps[:], gb_raw[:], ident_bf[:])
+                nc.scalar.copy(out=gb_col[:], in_=gb_ps[:])
+            if s == 2:
+                nc.vector.tensor_scalar(
+                    out=gb_col[:, 48:56], in0=gb_col[:, 48:56], scalar1=1.0, scalar2=None, op0=ALU.add
+                )
+            b_step(s)
+            matmuls(s, [4, 5, 6, 7])
+            cell_step(s - 1)
+            ve_pow(s - 1)
+
+        def back(k, a_t, m, plus, pool):
+            tag = "acc" if plus is not None else "bank"
+            bk0 = pool.tile([P, 512], F32, name="bk0", tag=tag)
+            bk1 = pool.tile([P, 512], F32, name="bk1", tag=tag)
+            halves_of[k] = [bk0[:], bk1[:]]
+            for j in range(JT):
+                dst = halves_of[k][j // 4][:, (j % 4) * P : (j % 4 + 1) * P]
+                if plus is None:
+                    nc.tensor.transpose(dst, a_t[:, j, m * P : (m + 1) * P], ident[:])
+                else:
+                    nc.tensor.matmul(
+                        out=dst, lhsT=a_t[:, j, m * P : (m + 1) * P], rhs=ident[:],
+                        start=True, stop=False, is_transpose=True,
+                    )
+                    nc.tensor.matmul(
+                        out=dst, lhsT=plus[:, j, m * P : (m + 1) * P], rhs=ident[:],
+                        start=False, stop=True, is_transpose=True,
+                    )
+
+        cy = {}
+        th = {}
+
+        def s_back(m):
+            back(16 + m, a_tiles[1], m, a_tiles[2], ps_acc)
+
+        def c_stats(ms):
+            for m in ms:
+                bn(16 + m)
+            for m in ms:
+                aggr(16 + m)
+            for m in ms:
+                flt(16 + m)
+            for m in ms:
+                ve_pow(16 + m)
+
+        def c_norm(m):
+            cy_t = work.tile([P, H], F32, name="cy_t", tag="w")
+            for h2 in range(2):
+                cols = slice(h2 * 512, (h2 + 1) * 512)
+                nc.vector.scalar_tensor_tensor(
+                    out=cy_t[:, cols], in0=halves_of[16 + m][h2], scalar=mv_of[16 + m][:, 0:1], in1=gam4[:, cols],
+                    op0=ALU.subtract, op1=ALU.mult,
+                )
+            nc.vector.scalar_tensor_tensor(
+                out=cy_t[:], in0=cy_t[:], scalar=rstd_of[16 + m][:], in1=bet4[:], op0=ALU.mult, op1=ALU.add
+            )
+            nc.sync.dma_start(out=out_2[m * P : (m + 1) * P, :], in_=cy_t[:])
+            th_t = nrm.tile([P, H], F32, name="th_t", tag="n")
+            nc.scalar.activation(out=th_t[:], in_=cy_t[:], func=ACT.Tanh)
+            th[m] = th_t
+
+        def o_back(m):
+            back(20 + m, a_tiles[3], m, None, ps_bank)
+
+        def finish(m):
+            hy_t = work.tile([P, H], F32, name="hy_t", tag="w")
+            for h2 in range(2):
+                cols = slice(h2 * 512, (h2 + 1) * 512)
+                nc.vector.tensor_tensor(out=hy_t[:, cols], in0=th[m][:, cols], in1=halves_of[20 + m][h2], op=ALU.mult)
+                nc.sync.dma_start(out=out_0[m * P : (m + 1) * P, cols], in_=hy_t[:, cols])
+                nc.sync.dma_start(out=out_1[m * P : (m + 1) * P, cols], in_=hy_t[:, cols])
+
+        def chain(k):
+            bn(k)
+            aggr(k)
+            flt(k)
+            ve_pow(k)
+
+        def close(k):
+            nmr(k)
+            normalise(k)
+
+        quant(12)
+        close(10)
+        matmuls(12, [0, 1, 2, 3])
+        chain(11)
+        b_step(12)
+        matmuls(12, [4, 5, 6, 7])
+        cell_step(11)
+        close(11)
+        matmuls(13, [0, 1, 2, 3])
+        chain(12)
+        b_step(13)
+        matmuls(13, [4, 5, 6, 7])
+        cell_step(12)
+        close(12)
+        matmuls(14, [0, 1, 2, 3])
+        chain(13)
+        b_step(14)
+        matmuls(14, [4, 5, 6, 7])
+        cell_step(13)
+        close(13)
+        s_back(0)
+        matmuls(15, [0, 1, 2, 3])
+        chain(14)
+        b_step(15)
+        cell_step(14)
+        close(14)
+        matmuls(15, [4, 5, 6, 7])
+        c_stats([0])
+        c_norm(0)
+        s_back(1)
+        chain(15)
+        cell_step(15)
+        close(15)
+        c_stats([1])
+        for jj in range(4):
+            ep(3, 0, jj)
+        s_back(2)
+        c_norm(1)
+        s_back(3)
+        o_back(0)
+        c_stats([2])
+        finish(0)
+        c_norm(2)
+        o_back(1)
+        c_stats([3])
+        finish(1)
+        for jj in range(4):
+            ep(3, 1, jj)
+        c_norm(3)
+        o_back(2)
+        finish(2)
+        o_back(3)
+        finish(3)

@@ -52,7 +52,7 @@ def tile_layernormdropoutlstmcell_kernel(
         wq = ctx.enter_context(tc.tile_pool(name="wq", bufs=2))
         nrm = ctx.enter_context(tc.tile_pool(name="nrm", bufs=6))
         gates = ctx.enter_context(tc.tile_pool(name="gates", bufs=3))
-        work = ctx.enter_context(tc.tile_pool(name="work", bufs=4))
+        work = ctx.enter_context(tc.tile_pool(name="work", bufs=5))
         small = ctx.enter_context(tc.tile_pool(name="small", bufs=8))
         ps_bank = ctx.enter_context(tc.psum_pool(name="ps_bank", bufs=3))
         ps_acc = ctx.enter_context(tc.psum_pool(name="ps_acc", bufs=5))
@@ -202,12 +202,13 @@ def tile_layernormdropoutlstmcell_kernel(
         def ok(k):
             return k in halves_of
 
-        def bn(k):
+        def bn(k, halves=(0, 1)):
             if ok(k):
-                st = small.tile([P, 2, 6], F32, name="st", tag="st")
-                for h2 in range(2):
-                    nc.vector.bn_stats(out=st[:, h2, :], in_=halves_of[k][h2])
-                st_of[k] = st
+                if halves[0] == 0:
+                    st = small.tile([P, 2, 6], F32, name="st", tag="st")
+                    st_of[k] = st
+                for h2 in halves:
+                    nc.vector.bn_stats(out=st_of[k][:, h2, :], in_=halves_of[k][h2])
 
         def aggr(k):
             if ok(k):
@@ -272,6 +273,8 @@ def tile_layernormdropoutlstmcell_kernel(
                 j = 2 * jj + j2
                 for m2 in range(2):
                     nc.tensor.transpose(bank[:, j2, m2, :], n_tiles[q][2 * pr + m2][:, j * P : (j + 1) * P], ident[:])
+            if q == 3:
+                a_tiles[3] = a_tiles[0]
             if q not in a_tiles:
                 a_new = gates.tile([P, JT, B], F32, name="a_t", tag="a")
                 a_tiles[q] = a_new
@@ -284,8 +287,8 @@ def tile_layernormdropoutlstmcell_kernel(
                     bias=gb_col[:, 40 + q * 8 + j : 41 + q * 8 + j],
                 )
 
-        def cell(q, pr, jh):
-            js = slice(4 * jh, 4 * jh + 4)
+        def cell(q, pr, jh, part=None):
+            js = slice(4 * jh, 4 * jh + 4) if part is None else slice(4 * jh + 2 * part, 4 * jh + 2 * part + 2)
             ts = slice(pr * 256, (pr + 1) * 256)
             if q == 1:
                 nc.vector.tensor_tensor(
@@ -311,10 +314,10 @@ def tile_layernormdropoutlstmcell_kernel(
                 ep(q, pr, 2 * jh)
                 ep(q, pr, 2 * jh + 1)
 
-        def cell_step(s):
+        def cell_step(s, part=None):
             if b_of(s) is not None:
                 q, pr, jh = b_of(s)
-                cell(q, pr, jh)
+                cell(q, pr, jh, part)
 
         for s in range(FIRST, 12):
             for w in LOADS.get(s, []):
@@ -384,32 +387,41 @@ def tile_layernormdropoutlstmcell_kernel(
             for m in ms:
                 ve_pow(16 + m)
 
-        def c_norm(m):
-            cy_t = work.tile([P, H], F32, name="cy_t", tag="w")
-            for h2 in range(2):
-                cols = slice(h2 * 512, (h2 + 1) * 512)
-                nc.vector.scalar_tensor_tensor(
-                    out=cy_t[:, cols], in0=halves_of[16 + m][h2], scalar=mv_of[16 + m][:, 0:1], in1=gam4[:, cols],
-                    op0=ALU.subtract, op1=ALU.mult,
-                )
+        def c_p1(m, h2):
+            if h2 == 0:
+                cy_t = work.tile([P, H], F32, name="cy_t", tag="w")
+                cy[m] = cy_t
+            cols = slice(h2 * 512, (h2 + 1) * 512)
             nc.vector.scalar_tensor_tensor(
-                out=cy_t[:], in0=cy_t[:], scalar=rstd_of[16 + m][:], in1=bet4[:], op0=ALU.mult, op1=ALU.add
+                out=cy[m][:, cols], in0=halves_of[16 + m][h2], scalar=mv_of[16 + m][:, 0:1], in1=gam4[:, cols],
+                op0=ALU.subtract, op1=ALU.mult,
             )
-            nc.sync.dma_start(out=out_2[m * P : (m + 1) * P, :], in_=cy_t[:])
-            th_t = nrm.tile([P, H], F32, name="th_t", tag="n")
-            nc.scalar.activation(out=th_t[:], in_=cy_t[:], func=ACT.Tanh)
-            th[m] = th_t
+
+        def c_p2(m, h2):
+            cols = slice(h2 * 512, (h2 + 1) * 512)
+            nc.vector.scalar_tensor_tensor(
+                out=cy[m][:, cols], in0=cy[m][:, cols], scalar=rstd_of[16 + m][:], in1=bet4[:, cols],
+                op0=ALU.mult, op1=ALU.add,
+            )
+            nc.sync.dma_start(out=out_2[m * P : (m + 1) * P, cols], in_=cy[m][:, cols])
+            if h2 == 0:
+                th_t = nrm.tile([P, H], F32, name="th_t", tag="n")
+                th[m] = th_t
+            nc.scalar.activation(out=th[m][:, cols], in_=cy[m][:, cols], func=ACT.Tanh)
 
         def o_back(m):
             back(20 + m, a_tiles[3], m, None, ps_bank)
 
-        def finish(m):
-            hy_t = work.tile([P, H], F32, name="hy_t", tag="w")
-            for h2 in range(2):
-                cols = slice(h2 * 512, (h2 + 1) * 512)
-                nc.vector.tensor_tensor(out=hy_t[:, cols], in0=th[m][:, cols], in1=halves_of[20 + m][h2], op=ALU.mult)
-                nc.sync.dma_start(out=out_0[m * P : (m + 1) * P, cols], in_=hy_t[:, cols])
-                nc.sync.dma_start(out=out_1[m * P : (m + 1) * P, cols], in_=hy_t[:, cols])
+        hy = {}
+
+        def fin(m, h2):
+            if h2 == 0:
+                hy_t = work.tile([P, H], F32, name="hy_t", tag="w")
+                hy[m] = hy_t
+            cols = slice(h2 * 512, (h2 + 1) * 512)
+            nc.vector.tensor_tensor(out=hy[m][:, cols], in0=th[m][:, cols], in1=halves_of[20 + m][h2], op=ALU.mult)
+            nc.sync.dma_start(out=out_0[m * P : (m + 1) * P, cols], in_=hy[m][:, cols])
+            nc.sync.dma_start(out=out_1[m * P : (m + 1) * P, cols], in_=hy[m][:, cols])
 
         def chain(k):
             bn(k)
@@ -421,56 +433,92 @@ def tile_layernormdropoutlstmcell_kernel(
             nmr(k)
             normalise(k)
 
+        A4 = [0, 1, 2, 3]
+        B4 = [4, 5, 6, 7]
         quant(12)
         close(10)
-        matmuls(12, [0, 1, 2, 3])
+        matmuls(12, A4)
         chain(11)
         b_step(12)
-        matmuls(12, [4, 5, 6, 7])
+        matmuls(12, B4)
         cell_step(11)
         close(11)
-        matmuls(13, [0, 1, 2, 3])
+        matmuls(13, A4)
         chain(12)
         b_step(13)
-        matmuls(13, [4, 5, 6, 7])
+        matmuls(13, B4)
         cell_step(12)
         close(12)
-        matmuls(14, [0, 1, 2, 3])
+        matmuls(14, A4)
         chain(13)
         b_step(14)
-        matmuls(14, [4, 5, 6, 7])
+        matmuls(14, B4)
         cell_step(13)
         close(13)
         s_back(0)
-        matmuls(15, [0, 1, 2, 3])
+        matmuls(15, A4)
         chain(14)
         b_step(15)
         cell_step(14)
         close(14)
-        matmuls(15, [4, 5, 6, 7])
-        c_stats([0])
-        c_norm(0)
-        s_back(1)
-        chain(15)
-        cell_step(15)
-        close(15)
-        c_stats([1])
+        matmuls(15, B4)
         for jj in range(4):
             ep(3, 0, jj)
-        s_back(2)
-        c_norm(1)
-        s_back(3)
+        bn(16)
+        bn(15, (0,))
+        aggr(16)
+        flt(16)
+        c_p1(0, 0)
+        ve_pow(16)
+        c_p1(0, 1)
+        s_back(1)
+        cell_step(15, 0)
+        cell_step(15, 1)
+        c_p2(0, 0)
+        bn(15, (1,))
+        c_p2(0, 1)
+        aggr(15)
         o_back(0)
-        c_stats([2])
-        finish(0)
-        c_norm(2)
-        o_back(1)
-        c_stats([3])
-        finish(1)
+        bn(17, (0,))
+        flt(15)
+        bn(17, (1,))
+        ve_pow(15)
+        fin(0, 0)
+        aggr(17)
+        fin(0, 1)
+        close(15)
+        flt(17)
+        c_p1(1, 0)
+        ve_pow(17)
+        c_p1(1, 1)
+        s_back(2)
         for jj in range(4):
             ep(3, 1, jj)
-        c_norm(3)
+        s_back(3)
+        o_back(1)
+        bn(18)
+        c_p2(1, 0)
+        aggr(18)
+        c_p2(1, 1)
+        flt(18)
+        c_p1(2, 0)
+        ve_pow(18)
+        c_p1(2, 1)
+        bn(19)
+        fin(1, 0)
+        aggr(19)
+        fin(1, 1)
+        flt(19)
+        c_p1(3, 0)
+        ve_pow(19)
+        c_p1(3, 1)
+        c_p2(2, 0)
+        c_p2(2, 1)
         o_back(2)
-        finish(2)
+        c_p2(3, 0)
+        c_p2(3, 1)
+        fin(2, 0)
+        fin(2, 1)
         o_back(3)
-        finish(3)
+        fin(3, 0)
+        fin(3, 1)

@@ -289,6 +289,8 @@ def tile_layernormdropoutlstmcell_kernel(
 
         def cell(q, pr, jh, part=None):
             js = slice(4 * jh, 4 * jh + 4) if part is None else slice(4 * jh + 2 * part, 4 * jh + 2 * part + 2)
+            if part is not None and part >= 10:
+                js = slice(4 * jh + part - 10, 4 * jh + part - 9)
             ts = slice(pr * 256, (pr + 1) * 256)
             if q == 1:
                 nc.vector.tensor_tensor(
@@ -438,42 +440,41 @@ def tile_layernormdropoutlstmcell_kernel(
         quant(12)
         close(10)
         matmuls(12, A4)
-        chain(11)
-        b_step(12)
-        matmuls(12, B4)
-        cell_step(11)
-        close(11)
-        matmuls(13, A4)
-        chain(12)
-        b_step(13)
-        matmuls(13, B4)
-        cell_step(12)
-        close(12)
-        matmuls(14, A4)
-        chain(13)
-        b_step(14)
-        matmuls(14, B4)
-        cell_step(13)
-        close(13)
-        s_back(0)
-        matmuls(15, A4)
-        chain(14)
-        b_step(15)
-        cell_step(14)
-        close(14)
-        matmuls(15, B4)
+        bn(11)
+        for s in (12, 13, 14, 15):
+            k = s - 1
+            if s > 12:
+                matmuls(s, A4)
+                bn(k, (1,))
+            cell_step(k, 10)
+            aggr(k)
+            cell_step(k, 11)
+            flt(k)
+            b_step(s)
+            if s < 15:
+                matmuls(s, B4)
+            cell_step(k, 12)
+            ve_pow(k)
+            cell_step(k, 13)
+            bn(s, (0,))
+            close(k)
+            if s == 14:
+                s_back(0)
+            if s == 15:
+                matmuls(s, B4)
         for jj in range(4):
             ep(3, 0, jj)
         bn(16)
-        bn(15, (0,))
+        cell_step(15, 10)
         aggr(16)
+        cell_step(15, 11)
         flt(16)
         c_p1(0, 0)
         ve_pow(16)
         c_p1(0, 1)
         s_back(1)
-        cell_step(15, 0)
-        cell_step(15, 1)
+        cell_step(15, 12)
+        cell_step(15, 13)
         c_p2(0, 0)
         bn(15, (1,))
         c_p2(0, 1)

@@ -64,6 +64,8 @@ def tile_layernormdropoutlstmcell_kernel(
 
         ctx.enter_context(tc.manual_schedule())
 
+        sc_raw = const.tile([P, P], F32, name="sc_raw")
+        nc.vector.memset(sc_raw[:], 0.0)
         neg_half = const.tile([P, 1], F32, name="neg_half")
         nc.vector.memset(neg_half[:], -0.5)
         zero_col = const.tile([P, 1], F32, name="zero_col")
@@ -73,8 +75,22 @@ def tile_layernormdropoutlstmcell_kernel(
         warm = const.tile([P, 1], F32, name="warm")
 
         sc_b = const.tile([P, I], F32, name="sc_b")
-        nc.scalar.dma_start(out=sc_b[:], in_=wih_scale.rearrange("o k -> (o k)").partition_broadcast(P))
+        nc.scalar.dma_start(out=sc_raw[0:8, :], in_=wih_scale.rearrange("o (c p) -> (o c) p", p=P))
         nc.scalar.activation(out=warm[:], in_=zero_col[:], func=ACT.Sigmoid)
+        sc_ps = ps_bank.tile([P, P], F32, name="sc_ps", tag="bank")
+        nc.tensor.transpose(sc_ps[:], sc_raw[:], ident[:])
+        sc_col = const.tile([P, 8], F32, name="sc_col")
+        nc.scalar.copy(out=sc_col[:], in_=sc_ps[:, 0:8])
+        for h2 in range(2):
+            sc_bank = ps_bank.tile([P, 512], F32, name="sc_bank", tag="bank")
+            for c4 in range(4):
+                nc.tensor.transpose(
+                    sc_bank[:, c4 * P : (c4 + 1) * P], sc_col[:, 4 * h2 + c4 : 4 * h2 + c4 + 1].to_broadcast([P, P]), ident[:]
+                )
+            if h2 == 0:
+                nc.scalar.copy(out=sc_b[:, 0:512], in_=sc_bank[:])
+            else:
+                nc.vector.tensor_copy(out=sc_b[:, 512:1024], in_=sc_bank[:])
 
         gam4 = const.tile([P, H], BF16, name="gam4")
         bet4 = const.tile([P, H], BF16, name="bet4")

@@ -20,21 +20,22 @@ JT = H // P
 FLOPS = 2 * B * 4 * H * (I + H)
 
 X_UNIT, HX_UNIT = -2, -1
-SEQ = [-2, -1, 1, 0, 2, 3, 5, 4, 6, 7, 9, 8, 10, 11, 13, 12, 14, 15]
+SEQ = [-2, -1, 1, 0, 2, 3] + list(range(4, 16))
 FIRST = -6
 TURN_AT = dict((FIRST + i, w) for i, w in enumerate(SEQ))
 STEP_OF = dict((w, s) for s, w in TURN_AT.items())
 LOADS = {
-    -6: [1, -2, "gb", -1, 3, 0, 2, 5],
+    -6: [1, -2, -1, 3, 0, 2, "gb", 5],
     -5: [4],
     -4: [6, 7],
-    -2: ["cx", 9],
-    -1: [8],
-    0: [11],
-    2: [10, 13],
-    3: [12],
-    4: [15],
-    6: [14, "g4"],
+    -2: ["cx"],
+    -1: [9],
+    0: [8],
+    1: [10, 11],
+    3: [12, 13],
+    4: [14],
+    5: [15],
+    6: ["g4"],
 }
 
 
@@ -134,16 +135,18 @@ def tile_layernormdropoutlstmcell_kernel(
         def widen_list(s):
             todo = []
             for w in (1, 3, 5, 7, 9, 11, 13, 15):
-                d = STEP_OF[w] - s - (1 if w % 4 == 3 else 0)
-                if d == 2:
+                first = -6 + w - 1 if w < 4 else max(STEP_OF[w] - 2, 0)
+                second = first + 1 if w < 4 else STEP_OF[w] - 1
+                if s == first:
                     todo = todo + [(w, 0), (w, 1)]
-                if d == 1:
+                if s == second:
                     todo = todo + [(w, 2), (w, 3)]
             return todo
 
         def widen(s, which):
             todo = widen_list(s)
-            for w, a in todo if which is None else todo[which : which + 1]:
+            n2 = len(todo) // 2
+            for w, a in todo if which is None else todo[which * n2 : (which + 1) * n2]:
                 wbf = wide.tile([P, 1024], BF16, name="wbf", tag="wbf")
                 nc.vector.tensor_tensor(out=wbf[:], in0=src[w][:, a, :].bitcast(FP8), in1=sc_b[:], op=ALU.mult)
                 views[w].append(wbf[:].bitcast(F32))
@@ -340,12 +343,12 @@ def tile_layernormdropoutlstmcell_kernel(
         for s in range(FIRST, 12):
             for w in LOADS.get(s, []):
                 load(w)
-            if s < -2:
+            if s < -4:
                 widen(s, None)
             bn(s - 1)
             nmr(s - 2)
             quant(s)
-            if -2 <= s < 0:
+            if -4 <= s < 0:
                 widen(s, None)
             aggr(s - 1)
             turn(s, True)

@@ -55,8 +55,25 @@ def tile_layernormdropoutlstmcell_kernel(
         gates = ctx.enter_context(tc.tile_pool(name="gates", bufs=3))
         work = ctx.enter_context(tc.tile_pool(name="work", bufs=5))
         small = ctx.enter_context(tc.tile_pool(name="small", bufs=8))
-        ps_bank = ctx.enter_context(tc.psum_pool(name="ps_bank", bufs=3))
-        ps_acc = ctx.enter_context(tc.psum_pool(name="ps_acc", bufs=5))
+        psum = ctx.enter_context(tc.psum_pool(name="psum", bufs=1))
+
+        def bank_tile(i, shape, dt, name):
+            t_new = psum.tile(shape, dt, name=name, tag="k%d" % i)
+            return t_new
+
+        turns = []
+
+        def t_bank(shape, dt, name):
+            turns.append(0)
+            ring = T_RING[0]
+            return bank_tile(ring[len(turns) % len(ring)], shape, dt, name)
+
+        T_RING = [(5, 6, 7)]
+
+        def acc_bank(s, half):
+            if s < 12:
+                return (2 * s + half) % 5
+            return (4, 7, 0, 1, 2, 3)[(2 * (s - 12) + half) % 6]
 
         ident = const.tile([P, P], F32, name="ident")
         make_identity(nc, ident[:])
@@ -78,12 +95,12 @@ def tile_layernormdropoutlstmcell_kernel(
         sc_b = const.tile([P, I], F32, name="sc_b")
         nc.scalar.dma_start(out=sc_raw[0:8, :], in_=wih_scale.rearrange("o (c p) -> (o c) p", p=P))
         nc.scalar.activation(out=warm[:], in_=zero_col[:], func=ACT.Sigmoid)
-        sc_ps = ps_bank.tile([P, P], F32, name="sc_ps", tag="bank")
+        sc_ps = t_bank([P, P], F32, "sc_ps")
         nc.tensor.transpose(sc_ps[:], sc_raw[:], ident[:])
         sc_col = const.tile([P, 8], F32, name="sc_col")
         nc.scalar.copy(out=sc_col[:], in_=sc_ps[:, 0:8])
         for h2 in range(2):
-            sc_bank = ps_bank.tile([P, 512], F32, name="sc_bank", tag="bank")
+            sc_bank = t_bank([P, 512], F32, "sc_bank")
             for c4 in range(4):
                 nc.tensor.transpose(
                     sc_bank[:, c4 * P : (c4 + 1) * P], sc_col[:, 4 * h2 + c4 : 4 * h2 + c4 + 1].to_broadcast([P, P]), ident[:]
@@ -160,7 +177,7 @@ def tile_layernormdropoutlstmcell_kernel(
                 grouped_of[w] = g_new
             gw = grouped_of[w][:].bitcast(F32)
             for a in (0, 1, 2) if first else (3,):
-                bank = ps_bank.tile([P, 2, 2, P], F32, name="bank", tag="bank")
+                bank = t_bank([P, 2, 2, P], F32, "bank")
                 for g in range(2):
                     for u in range(2):
                         nc.tensor.transpose(
@@ -194,7 +211,7 @@ def tile_layernormdropoutlstmcell_kernel(
             for p8 in passes:
                 half, c4 = p8 // 4, p8 % 4
                 if c4 == 0:
-                    acc_new = ps_acc.tile([P, 512], F32, name="acc", tag="acc")
+                    acc_new = bank_tile(acc_bank(s, half), [P, 512], F32, "acc")
                     if half == 0:
                         halves_of[s] = []
                     halves_of[s].append(acc_new[:])
@@ -276,7 +293,7 @@ def tile_layernormdropoutlstmcell_kernel(
                 n_tiles[s // 4].append(n_t)
 
         def ep_cx(jp):
-            bank = ps_bank.tile([P, 2, MT, P], BF16, name="cbank", tag="bank")
+            bank = t_bank([P, 2, MT, P], BF16, "cbank")
             for j2 in range(2):
                 j = 2 * jp + j2
                 for m in range(MT):
@@ -287,7 +304,7 @@ def tile_layernormdropoutlstmcell_kernel(
             )
 
         def ep(q, pr, jj):
-            bank = ps_bank.tile([P, 2, 2, P], F32, name="ebank", tag="bank")
+            bank = t_bank([P, 2, 2, P], F32, "ebank")
             for j2 in range(2):
                 j = 2 * jj + j2
                 for m2 in range(2):
@@ -361,7 +378,7 @@ def tile_layernormdropoutlstmcell_kernel(
             if s >= 0:
                 widen(s, 1)
             if s == 1:
-                gb_ps = ps_bank.tile([P, P], BF16, name="gb_ps", tag="bank")
+                gb_ps = t_bank([P, P], BF16, "gb_ps")
                 nc.tensor.transpose(gb_ps[:], gb_raw[:], ident_bf[:])
                 nc.scalar.copy(out=gb_col[:], in_=gb_ps[:])
             if s == 2:
@@ -373,10 +390,9 @@ def tile_layernormdropoutlstmcell_kernel(
             cell_step(s - 1)
             ve_pow(s - 1)
 
-        def back(k, a_t, m, plus, pool):
-            tag = "acc" if plus is not None else "bank"
-            bk0 = pool.tile([P, 512], F32, name="bk0", tag=tag)
-            bk1 = pool.tile([P, 512], F32, name="bk1", tag=tag)
+        def back(k, a_t, m, plus, two):
+            bk0 = bank_tile(two[0], [P, 512], F32, "bk0")
+            bk1 = bank_tile(two[1], [P, 512], F32, "bk1")
             halves_of[k] = [bk0[:], bk1[:]]
             for j in range(JT):
                 dst = halves_of[k][j // 4][:, (j % 4) * P : (j % 4 + 1) * P]
@@ -396,7 +412,7 @@ def tile_layernormdropoutlstmcell_kernel(
         th = {}
 
         def s_back(m):
-            back(16 + m, a_tiles[1], m, a_tiles[2], ps_acc)
+            back(16 + m, a_tiles[1], m, a_tiles[2], S_BANKS[m])
 
         def c_stats(ms):
             for m in ms:
@@ -431,7 +447,7 @@ def tile_layernormdropoutlstmcell_kernel(
             nc.scalar.activation(out=th[m][:, cols], in_=cy[m][:, cols], func=ACT.Tanh)
 
         def o_back(m):
-            back(20 + m, a_tiles[3], m, None, ps_bank)
+            back(20 + m, a_tiles[3], m, None, O_BANKS[m])
 
         hy = {}
 
@@ -456,6 +472,9 @@ def tile_layernormdropoutlstmcell_kernel(
 
         A4 = [0, 1, 2, 3]
         B4 = [4, 5, 6, 7]
+        S_BANKS = {0: (0, 1), 1: (2, 3), 2: (0, 1), 3: (2, 3)}
+        O_BANKS = {0: (5, 6), 1: (5, 6), 2: (4, 7), 3: (5, 6)}
+        T_RING[0] = (5, 6)
         quant(12)
         close(10)
         matmuls(12, A4)
@@ -464,23 +483,20 @@ def tile_layernormdropoutlstmcell_kernel(
             k = s - 1
             if s > 12:
                 matmuls(s, A4)
+                if s == 15:
+                    s_back(0)
                 bn(k, (1,))
             cell_step(k, 10)
             aggr(k)
             cell_step(k, 11)
             flt(k)
             b_step(s)
-            if s < 15:
-                matmuls(s, B4)
+            matmuls(s, B4)
             cell_step(k, 12)
             ve_pow(k)
             cell_step(k, 13)
             bn(s, (0,))
             close(k)
-            if s == 14:
-                s_back(0)
-            if s == 15:
-                matmuls(s, B4)
         for jj in range(4):
             ep(3, 0, jj)
         bn(16)
@@ -512,6 +528,7 @@ def tile_layernormdropoutlstmcell_kernel(
         ve_pow(17)
         c_p1(1, 1)
         s_back(2)
+        T_RING[0] = (4, 7)
         for jj in range(4):
             ep(3, 1, jj)
         s_back(3)

@@ -494,8 +494,8 @@ def tile_layernormdropoutlstmcell_kernel(
             matmuls(s, B4)
             cell_step(k, 12)
             ve_pow(k)
-            cell_step(k, 13)
             bn(s, (0,))
+            cell_step(k, 13)
             close(k)
         for jj in range(4):
             ep(3, 0, jj)

@@ -149,21 +149,19 @@ def tile_layernormdropoutlstmcell_kernel(
                 src[w] = wb
                 views[w] = []
 
+        WIDEN_COUNT = [4, 2, 2, 2, 3, 3, 2, 2, 2, 1, 1, 0]
+
         def widen_list(s):
-            todo = []
-            for w in (1, 3, 5, 7, 9, 11, 13, 15):
-                first = -6 + w - 1 if w < 4 else max(STEP_OF[w] - 2, 0)
-                second = first + 1 if w < 4 else STEP_OF[w] - 1
-                if s == first:
-                    todo = todo + [(w, 0), (w, 1)]
-                if s == second:
-                    todo = todo + [(w, 2), (w, 3)]
-            return todo
+            if s < 0:
+                return [[(1, 0), (1, 1)], [(1, 2), (1, 3)], [(3, 0), (3, 1)], [(3, 2), (3, 3)], [], []][s + 6]
+            rest = [(w, a) for w in (5, 7, 9, 11, 13, 15) for a in range(4)]
+            done = sum(WIDEN_COUNT[:s])
+            return rest[done : sum(WIDEN_COUNT[: s + 1])]
 
         def widen(s, which):
             todo = widen_list(s)
             n2 = len(todo) // 2
-            for w, a in todo if which is None else todo[which * n2 : (which + 1) * n2]:
+            for w, a in todo if which is None else (todo[n2:] if which else todo[:n2]):
                 wbf = wide.tile([P, 1024], BF16, name="wbf", tag="wbf")
                 nc.vector.tensor_tensor(out=wbf[:], in0=src[w][:, a, :].bitcast(FP8), in1=sc_b[:], op=ALU.mult)
                 views[w].append(wbf[:].bitcast(F32))
@@ -323,17 +321,17 @@ def tile_layernormdropoutlstmcell_kernel(
                     bias=gb_col[:, 40 + q * 8 + j : 41 + q * 8 + j],
                 )
 
-        def cell(q, pr, jh, part=None):
+        def cell(q, pr, jh, part=None, eng=None):
             js = slice(4 * jh, 4 * jh + 4) if part is None else slice(4 * jh + 2 * part, 4 * jh + 2 * part + 2)
             if part is not None and part >= 10:
                 js = slice(4 * jh + part - 10, 4 * jh + part - 9)
             ts = slice(pr * 256, (pr + 1) * 256)
             if q == 1:
-                nc.vector.tensor_tensor(
+                (eng or nc.vector).tensor_tensor(
                     out=a_tiles[1][:, js, ts], in0=a_tiles[1][:, js, ts], in1=cxT[:, js, ts], op=ALU.mult
                 )
             if q == 2:
-                nc.vector.tensor_tensor(
+                (eng or nc.vector).tensor_tensor(
                     out=a_tiles[2][:, js, ts], in0=a_tiles[2][:, js, ts], in1=a_tiles[0][:, js, ts], op=ALU.mult
                 )
 
@@ -352,10 +350,10 @@ def tile_layernormdropoutlstmcell_kernel(
                 ep(q, pr, 2 * jh)
                 ep(q, pr, 2 * jh + 1)
 
-        def cell_step(s, part=None):
+        def cell_step(s, part=None, eng=None):
             if b_of(s) is not None:
                 q, pr, jh = b_of(s)
-                cell(q, pr, jh, part)
+                cell(q, pr, jh, part, eng)
 
         for s in range(FIRST, 12):
             for w in LOADS.get(s, []):
@@ -387,8 +385,10 @@ def tile_layernormdropoutlstmcell_kernel(
                 )
             b_step(s)
             matmuls(s, [4, 5, 6, 7])
-            cell_step(s - 1)
+            cell_step(s - 1, 0)
+            cell_step(s - 1, 12)
             ve_pow(s - 1)
+            cell_step(s - 1, 13, nc.gpsimd)
 
         def back(k, a_t, m, plus, two):
             bk0 = bank_tile(two[0], [P, 512], F32, "bk0")
@@ -473,7 +473,7 @@ def tile_layernormdropoutlstmcell_kernel(
         A4 = [0, 1, 2, 3]
         B4 = [4, 5, 6, 7]
         S_BANKS = {0: (0, 1), 1: (2, 3), 2: (0, 1), 3: (2, 3)}
-        O_BANKS = {0: (5, 6), 1: (5, 6), 2: (4, 7), 3: (5, 6)}
+        O_BANKS = {0: (5, 6), 1: (4, 7), 2: (0, 1), 3: (2, 3)}
         T_RING[0] = (5, 6)
         quant(12)
         close(10)
@@ -494,11 +494,11 @@ def tile_layernormdropoutlstmcell_kernel(
             matmuls(s, B4)
             cell_step(k, 12)
             ve_pow(k)
+            cell_step(k, 13, nc.gpsimd)
             bn(s, (0,))
-            cell_step(k, 13)
             close(k)
-        for jj in range(4):
-            ep(3, 0, jj)
+        ep(3, 0, 0)
+        ep(3, 0, 1)
         bn(16)
         cell_step(15, 10)
         aggr(16)
@@ -506,56 +506,61 @@ def tile_layernormdropoutlstmcell_kernel(
         flt(16)
         c_p1(0, 0)
         ve_pow(16)
+        cell_step(15, 13, nc.gpsimd)
         c_p1(0, 1)
         s_back(1)
         cell_step(15, 12)
-        cell_step(15, 13)
-        c_p2(0, 0)
+        ep(3, 0, 2)
+        ep(3, 0, 3)
         bn(15, (1,))
-        c_p2(0, 1)
-        aggr(15)
-        o_back(0)
-        bn(17, (0,))
-        flt(15)
-        bn(17, (1,))
-        ve_pow(15)
-        fin(0, 0)
-        aggr(17)
-        fin(0, 1)
-        close(15)
-        flt(17)
-        c_p1(1, 0)
-        ve_pow(17)
-        c_p1(1, 1)
         s_back(2)
-        T_RING[0] = (4, 7)
-        for jj in range(4):
-            ep(3, 1, jj)
+        bn(17, (0,))
+        aggr(15)
+        bn(17, (1,))
+        flt(15)
+        aggr(17)
+        ve_pow(15)
+        c_p2(0, 0)
+        flt(17)
+        c_p2(0, 1)
+        ve_pow(17)
+        c_p1(1, 0)
+        c_p1(1, 1)
+        close(15)
+        o_back(0)
         s_back(3)
-        o_back(1)
-        bn(18)
+        bn(18, (0,))
+        fin(0, 0)
+        bn(18, (1,))
+        fin(0, 1)
         c_p2(1, 0)
         aggr(18)
         c_p2(1, 1)
+        o_back(1)
+        ep(3, 1, 0)
+        ep(3, 1, 1)
         flt(18)
         c_p1(2, 0)
         ve_pow(18)
         c_p1(2, 1)
-        bn(19)
+        ep(3, 1, 2)
+        ep(3, 1, 3)
         fin(1, 0)
-        aggr(19)
+        bn(19, (0,))
         fin(1, 1)
+        bn(19, (1,))
+        o_back(2)
+        c_p2(2, 0)
+        aggr(19)
+        c_p2(2, 1)
         flt(19)
         c_p1(3, 0)
         ve_pow(19)
         c_p1(3, 1)
-        c_p2(2, 0)
-        c_p2(2, 1)
-        o_back(2)
-        c_p2(3, 0)
-        c_p2(3, 1)
         fin(2, 0)
+        c_p2(3, 0)
         fin(2, 1)
+        c_p2(3, 1)
         o_back(3)
         fin(3, 0)
         fin(3, 1)

@@ -93,7 +93,7 @@ def tile_layernormdropoutlstmcell_kernel(
         warm = const.tile([P, 1], F32, name="warm")
 
         sc_b = const.tile([P, I], F32, name="sc_b")
-        nc.scalar.dma_start(out=sc_raw[0:8, :], in_=wih_scale.rearrange("o (c p) -> (o c) p", p=P))
+        nc.sync.dma_start(out=sc_raw[0:8, :], in_=wih_scale.rearrange("o (c p) -> (o c) p", p=P))
         nc.scalar.activation(out=warm[:], in_=zero_col[:], func=ACT.Sigmoid)
         sc_ps = t_bank([P, P], F32, "sc_ps")
         nc.tensor.transpose(sc_ps[:], sc_raw[:], ident[:])

@@ -24,6 +24,7 @@ SEQ = [-2, -1, 1, 0, 2, 3] + list(range(4, 16))
 FIRST = -6
 TURN_AT = dict((FIRST + i, w) for i, w in enumerate(SEQ))
 STEP_OF = dict((w, s) for s, w in TURN_AT.items())
+FIRST_BYTES = {X_UNIT: {0: 0, 1: 1, 3: 2}, HX_UNIT: {0: 3}}
 LOADS = {
     -6: [1, -2, -1, 3, 0, 2, "gb", 5],
     -5: [4],
@@ -105,10 +106,7 @@ def tile_layernormdropoutlstmcell_kernel(
                 nc.tensor.transpose(
                     sc_bank[:, c4 * P : (c4 + 1) * P], sc_col[:, 4 * h2 + c4 : 4 * h2 + c4 + 1].to_broadcast([P, P]), ident[:]
                 )
-            if h2 == 0:
-                nc.scalar.copy(out=sc_b[:, 0:512], in_=sc_bank[:])
-            else:
-                nc.vector.tensor_copy(out=sc_b[:, 512:1024], in_=sc_bank[:])
+            nc.scalar.copy(out=sc_b[:, h2 * 512 : (h2 + 1) * 512], in_=sc_bank[:])
 
         gam4 = const.tile([P, H], BF16, name="gam4")
         bet4 = const.tile([P, H], BF16, name="bet4")
@@ -136,6 +134,9 @@ def tile_layernormdropoutlstmcell_kernel(
                 rows = cx if w == "cx" else (x if w == X_UNIT else (hx if w == HX_UNIT else whh[w_rows(w), :]))
                 if w != "cx" and w < 0:
                     for a in range(4):
+                        if a in FIRST_BYTES[w]:
+                            b = FIRST_BYTES[w][a]
+                            nc.sync.dma_start(out=src[1][:, b, :], in_=wih_bytes[b * P : (b + 1) * P, :])
                         nc.sync.dma_start(out=raw[:, a, :], in_=rows[a * P : (a + 1) * P, :])
                 else:
                     nc.sync.dma_start(out=raw[:], in_=rows.rearrange("(a p) k -> p a k", p=P))
@@ -145,7 +146,8 @@ def tile_layernormdropoutlstmcell_kernel(
                     views[w] = [words[:, a, :] for a in range(4)]
             else:
                 wb = bytes_pool.tile([P, 4, 1024], U8, name="wb", tag="wb")
-                nc.sync.dma_start(out=wb[:], in_=wih_bytes[w_rows(w), :].rearrange("(a p) k -> p a k", p=P))
+                if w > 1:
+                    nc.sync.dma_start(out=wb[:], in_=wih_bytes[w_rows(w), :].rearrange("(a p) k -> p a k", p=P))
                 src[w] = wb
                 views[w] = []
 
@@ -163,7 +165,10 @@ def tile_layernormdropoutlstmcell_kernel(
             n2 = len(todo) // 2
             for w, a in todo if which is None else (todo[n2:] if which else todo[:n2]):
                 wbf = wide.tile([P, 1024], BF16, name="wbf", tag="wbf")
-                nc.vector.tensor_tensor(out=wbf[:], in0=src[w][:, a, :].bitcast(FP8), in1=sc_b[:], op=ALU.mult)
+                for cols in (slice(0, 512), slice(512, 1024)) if (w, a) == (1, 0) else (slice(0, 1024),):
+                    nc.vector.tensor_tensor(
+                        out=wbf[:, cols], in0=src[w][:, a, cols].bitcast(FP8), in1=sc_b[:, cols], op=ALU.mult
+                    )
                 views[w].append(wbf[:].bitcast(F32))
 
         def turn(s, first):
@@ -181,7 +186,7 @@ def tile_layernormdropoutlstmcell_kernel(
                         nc.tensor.transpose(
                             bank[:, g, u, :], views[w][a][:, 256 * g + u : 256 * (g + 1) : 2], ident[:]
                         )
-                nc.scalar.copy(
+                (nc.vector.tensor_copy if s == -1 and a == 3 else nc.scalar.copy)(
                     out=gw[:, :, a * P : (a + 1) * P, :], in_=bank[:].rearrange("p g u r -> p g r u")
                 )
 

@@ -76,10 +76,10 @@ def tile_layernormdropoutlstmcell_kernel(
                 return (2 * s + half) % 5
             return (4, 7, 0, 1, 2, 3)[(2 * (s - 12) + half) % 6]
 
-        ident = const.tile([P, P], F32, name="ident")
-        make_identity(nc, ident[:])
         ident_bf = const.tile([P, P], BF16, name="ident_bf")
         make_identity(nc, ident_bf[:])
+        ident = const.tile([P, P], F32, name="ident")
+        make_identity(nc, ident[:])
 
         ctx.enter_context(tc.manual_schedule())
 
@@ -96,6 +96,9 @@ def tile_layernormdropoutlstmcell_kernel(
         sc_b = const.tile([P, I], F32, name="sc_b")
         nc.sync.dma_start(out=sc_raw[0:8, :], in_=wih_scale.rearrange("o (c p) -> (o c) p", p=P))
         nc.scalar.activation(out=warm[:], in_=zero_col[:], func=ACT.Sigmoid)
+        idle = bank_tile(0, [P, P], F32, "idle")
+        for i in range(10):
+            nc.tensor.matmul(out=idle[:], lhsT=ident_bf[:], rhs=ident_bf[:], start=True, stop=True)
         sc_ps = t_bank([P, P], F32, "sc_ps")
         nc.tensor.transpose(sc_ps[:], sc_raw[:], ident[:])
         sc_col = const.tile([P, 8], F32, name="sc_col")
@@ -390,10 +393,8 @@ def tile_layernormdropoutlstmcell_kernel(
                 )
             b_step(s)
             matmuls(s, [4, 5, 6, 7])
-            cell_step(s - 1, 0)
-            cell_step(s - 1, 12)
+            cell_step(s - 1)
             ve_pow(s - 1)
-            cell_step(s - 1, 13, nc.gpsimd)
 
         def back(k, a_t, m, plus, two):
             bk0 = bank_tile(two[0], [P, 512], F32, "bk0")

@@ -165,7 +165,7 @@ def tile_layernormdropoutlstmcell_kernel(
 
         def widen(s, which):
             todo = widen_list(s)
-            n2 = len(todo) // 2
+            n2 = (len(todo) + 1) // 2
             for w, a in todo if which is None else (todo[n2:] if which else todo[:n2]):
                 wbf = wide.tile([P, 1024], BF16, name="wbf", tag="wbf")
                 for cols in (slice(0, 512), slice(512, 1024)) if (w, a) == (1, 0) else (slice(0, 1024),):
@@ -379,6 +379,8 @@ def tile_layernormdropoutlstmcell_kernel(
             matmuls(s, [0, 1, 2, 3])
             if s >= 0:
                 widen(s, 0)
+            if s == 11:
+                cell_step(s - 1, 0)
             flt(s - 1)
             turn(s, False)
             if s >= 0:
@@ -393,7 +395,7 @@ def tile_layernormdropoutlstmcell_kernel(
                 )
             b_step(s)
             matmuls(s, [4, 5, 6, 7])
-            cell_step(s - 1)
+            cell_step(s - 1, 1 if s == 11 else None)
             ve_pow(s - 1)
 
         def back(k, a_t, m, plus, two):
@@ -481,10 +483,11 @@ def tile_layernormdropoutlstmcell_kernel(
         S_BANKS = {0: (0, 1), 1: (2, 3), 2: (0, 1), 3: (2, 3)}
         O_BANKS = {0: (5, 6), 1: (4, 7), 2: (0, 1), 3: (2, 3)}
         T_RING[0] = (5, 6)
+        bn(11, (0,))
         quant(12)
         close(10)
         matmuls(12, A4)
-        bn(11)
+        bn(11, (1,))
         for s in (12, 13, 14, 15):
             k = s - 1
             if s > 12:
@@ -515,57 +518,57 @@ def tile_layernormdropoutlstmcell_kernel(
         cell_step(15, 13, nc.gpsimd)
         c_p1(0, 1)
         s_back(1)
-        cell_step(15, 12)
         ep(3, 0, 2)
         ep(3, 0, 3)
         bn(15, (1,))
-        s_back(2)
         bn(17, (0,))
+        cell_step(15, 12)
+        s_back(2)
         aggr(15)
-        bn(17, (1,))
-        flt(15)
-        aggr(17)
-        ve_pow(15)
         c_p2(0, 0)
-        flt(17)
+        flt(15)
+        bn(17, (1,))
+        ve_pow(15)
+        aggr(17)
         c_p2(0, 1)
-        ve_pow(17)
+        flt(17)
         c_p1(1, 0)
+        ve_pow(17)
         c_p1(1, 1)
         close(15)
         o_back(0)
         s_back(3)
         bn(18, (0,))
         fin(0, 0)
-        bn(18, (1,))
         fin(0, 1)
         c_p2(1, 0)
-        aggr(18)
         c_p2(1, 1)
+        bn(18, (1,))
         o_back(1)
         ep(3, 1, 0)
         ep(3, 1, 1)
+        aggr(18)
+        fin(1, 0)
         flt(18)
         c_p1(2, 0)
         ve_pow(18)
         c_p1(2, 1)
         ep(3, 1, 2)
         ep(3, 1, 3)
-        fin(1, 0)
-        bn(19, (0,))
         fin(1, 1)
-        bn(19, (1,))
-        o_back(2)
+        bn(19, (0,))
         c_p2(2, 0)
-        aggr(19)
+        bn(19, (1,))
         c_p2(2, 1)
+        o_back(2)
+        aggr(19)
+        fin(2, 0)
         flt(19)
         c_p1(3, 0)
         ve_pow(19)
         c_p1(3, 1)
-        fin(2, 0)
-        c_p2(3, 0)
         fin(2, 1)
+        c_p2(3, 0)
         c_p2(3, 1)
         o_back(3)
         fin(3, 0)

from contextlib import ExitStack

import concourse.mybir as mybir
from concourse.masks import make_identity

F32 = mybir.dt.float32
BF16 = mybir.dt.bfloat16
U32 = mybir.dt.uint32
U8 = mybir.dt.uint8
FP8 = mybir.dt.float8_e4m3fn
FP8X4 = mybir.dt.float8_e4m3fn_x4
ALU = mybir.AluOpType
ACT = mybir.ActivationFunctionType

B, I, H = 512, 1024, 1024
EPS = 1e-12
P = 128
MT = B // P
JT = H // P
FLOPS = 2 * B * 4 * H * (I + H)

X_UNIT, HX_UNIT = -2, -1
SEQ = [-2, -1, 1, 0, 2, 3] + list(range(4, 16))
FIRST = -6
TURN_AT = dict((FIRST + i, w) for i, w in enumerate(SEQ))
STEP_OF = dict((w, s) for s, w in TURN_AT.items())
FIRST_BYTES = {X_UNIT: {0: 0, 1: 1, 3: 2}, HX_UNIT: {0: 3}}
LOADS = {
    -6: [1, -2, -1, 3, 0, 2, "gb", 5],
    -5: [4],
    -4: [6, 7],
    -2: ["cx"],
    -1: [9],
    0: [8],
    1: [10, 11],
    3: [12, 13],
    4: [14],
    5: [15],
    6: ["g4"],
}


def tile_layernormdropoutlstmcell_kernel(
    tc, x, hx, cx, wih_bytes, wih_scale, whh, gamma, beta, out_0, out_1, out_2
):
    nc = tc.nc
    with ExitStack() as ctx:
        const = ctx.enter_context(tc.tile_pool(name="const", bufs=1))
        stage = ctx.enter_context(tc.tile_pool(name="stage", bufs=4))
        bytes_pool = ctx.enter_context(tc.tile_pool(name="bytesp", bufs=3))
        wide = ctx.enter_context(tc.tile_pool(name="wide", bufs=8))
        grp = ctx.enter_context(tc.tile_pool(name="grp", bufs=2))
        keep = ctx.enter_context(tc.tile_pool(name="keep", bufs=1))
        wq = ctx.enter_context(tc.tile_pool(name="wq", bufs=2))
        nrm = ctx.enter_context(tc.tile_pool(name="nrm", bufs=6))
        gates = ctx.enter_context(tc.tile_pool(name="gates", bufs=3))
        work = ctx.enter_context(tc.tile_pool(name="work", bufs=5))
        small = ctx.enter_context(tc.tile_pool(name="small", bufs=8))
        psum = ctx.enter_context(tc.psum_pool(name="psum", bufs=1))

        def bank_tile(i, shape, dt, name):
            t_new = psum.tile(shape, dt, name=name, tag="k%d" % i)
            return t_new

        turns = []

        def t_bank(shape, dt, name):
            turns.append(0)
            ring = T_RING[0]
            return bank_tile(ring[len(turns) % len(ring)], shape, dt, name)

        T_RING = [(5, 6, 7)]

        def acc_bank(s, half):
            if s < 12:
                return (2 * s + half) % 5
            return (4, 7, 0, 1, 2, 3)[(2 * (s - 12) + half) % 6]

        ident_bf = const.tile([P, P], BF16, name="ident_bf")
        make_identity(nc, ident_bf[:])
        ident = const.tile([P, P], F32, name="ident")
        make_identity(nc, ident[:])

        ctx.enter_context(tc.manual_schedule())

        sc_raw = const.tile([P, P], F32, name="sc_raw")
        nc.vector.memset(sc_raw[:], 0.0)
        neg_half = const.tile([P, 1], F32, name="neg_half")
        nc.vector.memset(neg_half[:], -0.5)
        zero_col = const.tile([P, 1], F32, name="zero_col")
        nc.vector.memset(zero_col[:], 0.0)
        gb_raw = const.tile([P, P], BF16, name="gb_raw")
        nc.vector.memset(gb_raw[:], 0.0)
        warm = const.tile([P, 1], F32, name="warm")

        sc_b = const.tile([P, I], F32, name="sc_b")
        nc.sync.dma_start(out=sc_raw[0:8, :], in_=wih_scale.rearrange("o (c p) -> (o c) p", p=P))
        nc.scalar.activation(out=warm[:], in_=zero_col[:], func=ACT.Sigmoid)
        idle = bank_tile(0, [P, P], F32, "idle")
        for i in range(10):
            nc.tensor.matmul(out=idle[:], lhsT=ident_bf[:], rhs=ident_bf[:], start=True, stop=True)
        sc_ps = t_bank([P, P], F32, "sc_ps")
        nc.tensor.transpose(sc_ps[:], sc_raw[:], ident[:])
        sc_col = const.tile([P, 8], F32, name="sc_col")
        nc.scalar.copy(out=sc_col[:], in_=sc_ps[:, 0:8])
        for h2 in range(2):
            sc_bank = t_bank([P, 512], F32, "sc_bank")
            for c4 in range(4):
                nc.tensor.transpose(
                    sc_bank[:, c4 * P : (c4 + 1) * P], sc_col[:, 4 * h2 + c4 : 4 * h2 + c4 + 1].to_broadcast([P, P]), ident[:]
                )
            nc.scalar.copy(out=sc_b[:, h2 * 512 : (h2 + 1) * 512], in_=sc_bank[:])

        gam4 = const.tile([P, H], BF16, name="gam4")
        bet4 = const.tile([P, H], BF16, name="bet4")
        gb_col = const.tile([P, P], F32, name="gb_col")
        cxT = const.tile([P, JT, B], BF16, name="cxT")

        src = {}
        views = {}
        grouped_of = {}
        codes = {}

        def w_rows(w):
            r0 = (w // 4) * H + ((w % 4) // 2) * 512
            return slice(r0, r0 + 512)

        def load(w):
            if w == "gb":
                nc.sync.dma_start(out=gb_raw[0:40, :], in_=gamma.rearrange("a (j c) -> (a j) c", c=P))
                nc.sync.dma_start(out=gb_raw[40:80, :], in_=beta.rearrange("a (j c) -> (a j) c", c=P))
            elif w == "g4":
                nc.sync.dma_start(out=gam4[:], in_=gamma[4:5, :].rearrange("a h -> (a h)").partition_broadcast(P))
                nc.sync.dma_start(out=bet4[:], in_=beta[4:5, :].rearrange("a h -> (a h)").partition_broadcast(P))
            elif w == "cx" or w < 0 or w % 2 == 0:
                raw = stage.tile([P, 4, 1024], BF16, name="raw", tag="raw")
                rows = cx if w == "cx" else (x if w == X_UNIT else (hx if w == HX_UNIT else whh[w_rows(w), :]))
                if w != "cx" and w < 0:
                    for a in range(4):
                        if a in FIRST_BYTES[w]:
                            b = FIRST_BYTES[w][a]
                            nc.sync.dma_start(out=src[1][:, b, :], in_=wih_bytes[b * P : (b + 1) * P, :])
                        nc.sync.dma_start(out=raw[:, a, :], in_=rows[a * P : (a + 1) * P, :])
                else:
                    nc.sync.dma_start(out=raw[:], in_=rows.rearrange("(a p) k -> p a k", p=P))
                src[w] = raw
                if w != "cx":
                    words = raw[:].bitcast(F32)
                    views[w] = [words[:, a, :] for a in range(4)]
            else:
                wb = bytes_pool.tile([P, 4, 1024], U8, name="wb", tag="wb")
                if w > 1:
                    nc.sync.dma_start(out=wb[:], in_=wih_bytes[w_rows(w), :].rearrange("(a p) k -> p a k", p=P))
                src[w] = wb
                views[w] = []

        WIDEN_COUNT = [4, 2, 2, 2, 3, 3, 2, 2, 2, 1, 1, 0]

        def widen_list(s):
            if s < 0:
                return [[(1, 0), (1, 1)], [(1, 2), (1, 3)], [(3, 0), (3, 1)], [(3, 2), (3, 3)], [], []][s + 6]
            rest = [(w, a) for w in (5, 7, 9, 11, 13, 15) for a in range(4)]
            done = sum(WIDEN_COUNT[:s])
            return rest[done : sum(WIDEN_COUNT[: s + 1])]

        def widen(s, which):
            todo = widen_list(s)
            n2 = (len(todo) + 1) // 2
            for w, a in todo if which is None else (todo[n2:] if which else todo[:n2]):
                wbf = wide.tile([P, 1024], BF16, name="wbf", tag="wbf")
                for cols in (slice(0, 512), slice(512, 1024)) if (w, a) == (1, 0) else (slice(0, 1024),):
                    nc.vector.tensor_tensor(
                        out=wbf[:, cols], in0=src[w][:, a, cols].bitcast(FP8), in1=sc_b[:, cols], op=ALU.mult
                    )
                views[w].append(wbf[:].bitcast(F32))

        def turn(s, first):
            if s not in TURN_AT:
                return
            w = TURN_AT[s]
            if first:
                g_new = grp.tile([P, 2, 512, 4], BF16, name="grouped", tag="grouped", align_bytes=64)
                grouped_of[w] = g_new
            gw = grouped_of[w][:].bitcast(F32)
            for a in (0, 1, 2) if first else (3,):
                bank = t_bank([P, 2, 2, P], F32, "bank")
                for g in range(2):
                    for u in range(2):
                        nc.tensor.transpose(
                            bank[:, g, u, :], views[w][a][:, 256 * g + u : 256 * (g + 1) : 2], ident[:]
                        )
                (nc.vector.tensor_copy if s == -1 and a == 3 else nc.scalar.copy)(
                    out=gw[:, :, a * P : (a + 1) * P, :], in_=bank[:].rearrange("p g u r -> p g r u")
                )

        def quant(s):
            if s - 1 not in TURN_AT:
                return
            w = TURN_AT[s - 1]
            if w < 0:
                c = keep.tile([P, 1024], U32, name="ac%d" % (w + 2), align_bytes=64)
                s = keep.tile([P, 1024], U8, name="as%d" % (w + 2), align_bytes=64)
            else:
                c = wq.tile([P, 1024], U32, name="wc%d" % (w % 4), tag="wc%d" % (w % 4), align_bytes=64)
                s = wq.tile([P, 1024], U8, name="ws%d" % (w % 4), tag="ws%d" % (w % 4), align_bytes=64)
            nc.vector.quantize_mx(
                out=c[:].bitcast(FP8X4), scales=s[:], in_=grouped_of[w][:].rearrange("p g n t -> p (g n t)")
            )
            codes[w] = (c, s)

        halves_of = {}

        def matmuls(s, passes):
            if not 0 <= s <= 15:
                return
            q, m = s // 4, s % 4
            for p8 in passes:
                half, c4 = p8 // 4, p8 % 4
                if c4 == 0:
                    acc_new = bank_tile(acc_bank(s, half), [P, 512], F32, "acc")
                    if half == 0:
                        halves_of[s] = []
                    halves_of[s].append(acc_new[:])
                mat, g = 1 - c4 // 2, c4 % 2
                wc, ws = codes[4 * q + 2 * half + (1 - mat)]
                ac, asc = codes[X_UNIT + mat]
                cols = slice(g * 512 + m * P, g * 512 + (m + 1) * P)
                nc.tensor.matmul_mx(
                    out=halves_of[s][half],
                    lhsT=ac[:, cols].bitcast(FP8X4),
                    lhsT_scale=asc[:, cols],
                    rhs=wc[:, g * 512 : (g + 1) * 512].bitcast(FP8X4),
                    rhs_scale=ws[:, g * 512 : (g + 1) * 512],
                    start=(c4 == 0),
                    stop=(c4 == 3),
                )

        st_of = {}
        mv_of = {}
        flt_of = {}
        rstd_of = {}
        nmr_of = {}

        def ok(k):
            return k in halves_of

        def bn(k, halves=(0, 1)):
            if ok(k):
                if halves[0] == 0:
                    st = small.tile([P, 2, 6], F32, name="st", tag="st")
                    st_of[k] = st
                for h2 in halves:
                    nc.vector.bn_stats(out=st_of[k][:, h2, :], in_=halves_of[k][h2])

        def aggr(k):
            if ok(k):
                mv = small.tile([P, 2], F32, name="mv", tag="mv")
                nc.vector.bn_aggr(out=mv[:], in_=st_of[k][:].rearrange("p a b -> p (a b)"))
                mv_of[k] = mv

        def flt(k):
            if ok(k):
                f = small.tile([P, 1], F32, name="flt", tag="flt")
                nc.vector.tensor_scalar(
                    out=f[:], in0=mv_of[k][:, 1:2], scalar1=EPS, scalar2=0.01, op0=ALU.is_lt, op1=ALU.mult
                )
                flt_of[k] = f

        def ve_pow(k):
            if ok(k):
                ve = small.tile([P, 1], F32, name="ve", tag="ve")
                nc.vector.scalar_tensor_tensor(
                    out=ve[:], in0=mv_of[k][:, 1:2], scalar=EPS, in1=flt_of[k][:], op0=ALU.add, op1=ALU.add
                )
                rstd = small.tile([P, 1], F32, name="rstd", tag="rstd")
                nc.gpsimd.tensor_tensor(out=rstd[:], in0=ve[:], in1=neg_half[:], op=ALU.pow)
                rstd_of[k] = rstd

        def nmr(k):
            if ok(k):
                t = small.tile([P, 1], F32, name="nmr", tag="nmr")
                nc.vector.tensor_scalar(
                    out=t[:], in0=mv_of[k][:, 0:1], scalar1=rstd_of[k][:], scalar2=-1.0, op0=ALU.mult, op1=ALU.mult
                )
                nmr_of[k] = t

        n_tiles = {0: [], 1: [], 2: [], 3: []}
        a_tiles = {}
        FUNC = [ACT.Sigmoid, ACT.Sigmoid, ACT.Tanh, ACT.Sigmoid]

        def normalise(s):
            if ok(s):
                n_t = nrm.tile([P, H], F32, name="n_t", tag="n")
                for h2 in range(2):
                    nc.scalar.activation(
                        out=n_t[:, h2 * 512 : (h2 + 1) * 512], in_=halves_of[s][h2], func=ACT.Identity,
                        scale=rstd_of[s][:], bias=nmr_of[s][:],
                    )
                n_tiles[s // 4].append(n_t)

        def ep_cx(jp):
            bank = t_bank([P, 2, MT, P], BF16, "cbank")
            for j2 in range(2):
                j = 2 * jp + j2
                for m in range(MT):
                    nc.tensor.transpose(bank[:, j2, m, :], src["cx"][:, m, j * P : (j + 1) * P], ident_bf[:])
            nc.scalar.copy(
                out=cxT[:, 2 * jp : 2 * jp + 2, :].rearrange("p j t -> p (j t)"),
                in_=bank[:].rearrange("p j m t -> p (j m t)"),
            )

        def ep(q, pr, jj):
            bank = t_bank([P, 2, 2, P], F32, "ebank")
            for j2 in range(2):
                j = 2 * jj + j2
                for m2 in range(2):
                    nc.tensor.transpose(bank[:, j2, m2, :], n_tiles[q][2 * pr + m2][:, j * P : (j + 1) * P], ident[:])
            if q == 3:
                a_tiles[3] = a_tiles[0]
            if q not in a_tiles:
                a_new = gates.tile([P, JT, B], F32, name="a_t", tag="a")
                a_tiles[q] = a_new
            for j2 in range(2):
                j = 2 * jj + j2
                nc.scalar.activation(
                    out=a_tiles[q][:, j, pr * 256 : (pr + 1) * 256],
                    in_=bank[:, j2, :, :].rearrange("p m t -> p (m t)"), func=FUNC[q],
                    scale=gb_col[:, q * 8 + j : q * 8 + j + 1],
                    bias=gb_col[:, 40 + q * 8 + j : 41 + q * 8 + j],
                )

        def cell(q, pr, jh, part=None, eng=None):
            js = slice(4 * jh, 4 * jh + 4) if part is None else slice(4 * jh + 2 * part, 4 * jh + 2 * part + 2)
            if part is not None and part >= 10:
                js = slice(4 * jh + part - 10, 4 * jh + part - 9)
            ts = slice(pr * 256, (pr + 1) * 256)
            if q == 1:
                (eng or nc.vector).tensor_tensor(
                    out=a_tiles[1][:, js, ts], in0=a_tiles[1][:, js, ts], in1=cxT[:, js, ts], op=ALU.mult
                )
            if q == 2:
                (eng or nc.vector).tensor_tensor(
                    out=a_tiles[2][:, js, ts], in0=a_tiles[2][:, js, ts], in1=a_tiles[0][:, js, ts], op=ALU.mult
                )

        CX_AT = {1: [0], 2: [1], 3: [2, 3]}

        def b_of(s):
            if 4 <= s <= 15:
                return ((s - 4) // 4, ((s - 4) % 4) // 2, (s - 4) % 2)
            return None

        def b_step(s):
            for j in CX_AT.get(s, []):
                ep_cx(j)
            if b_of(s) is not None:
                q, pr, jh = b_of(s)
                ep(q, pr, 2 * jh)
                ep(q, pr, 2 * jh + 1)

        def cell_step(s, part=None, eng=None):
            if b_of(s) is not None:
                q, pr, jh = b_of(s)
                cell(q, pr, jh, part, eng)

        for s in range(FIRST, 12):
            for w in LOADS.get(s, []):
                load(w)
            if s < -4:
                widen(s, None)
            bn(s - 1)
            nmr(s - 2)
            quant(s)
            if -4 <= s < 0:
                widen(s, None)
            aggr(s - 1)
            turn(s, True)
            normalise(s - 2)
            matmuls(s, [0, 1, 2, 3])
            if s >= 0:
                widen(s, 0)
            if s == 11:
                cell_step(s - 1, 0)
            flt(s - 1)
            turn(s, False)
            if s >= 0:
                widen(s, 1)
            if s == 1:
                gb_ps = t_bank([P, P], BF16, "gb_ps")
                nc.tensor.transpose(gb_ps[:], gb_raw[:], ident_bf[:])
                nc.scalar.copy(out=gb_col[:], in_=gb_ps[:])
            if s == 2:
                nc.vector.tensor_scalar(
                    out=gb_col[:, 48:56], in0=gb_col[:, 48:56], scalar1=1.0, scalar2=None, op0=ALU.add
                )
            b_step(s)
            matmuls(s, [4, 5, 6, 7])
            cell_step(s - 1, 1 if s == 11 else None)
            ve_pow(s - 1)

        def back(k, a_t, m, plus, two):
            bk0 = bank_tile(two[0], [P, 512], F32, "bk0")
            bk1 = bank_tile(two[1], [P, 512], F32, "bk1")
            halves_of[k] = [bk0[:], bk1[:]]
            for j in range(JT):
                dst = halves_of[k][j // 4][:, (j % 4) * P : (j % 4 + 1) * P]
                if plus is None:
                    nc.tensor.transpose(dst, a_t[:, j, m * P : (m + 1) * P], ident[:])
                else:
                    nc.tensor.matmul(
                        out=dst, lhsT=a_t[:, j, m * P : (m + 1) * P], rhs=ident[:],
                        start=True, stop=False, is_transpose=True,
                    )
                    nc.tensor.matmul(
                        out=dst, lhsT=plus[:, j, m * P : (m + 1) * P], rhs=ident[:],
                        start=False, stop=True, is_transpose=True,
                    )

        cy = {}
        th = {}

        def s_back(m):
            back(16 + m, a_tiles[1], m, a_tiles[2], S_BANKS[m])

        def c_stats(ms):
            for m in ms:
                bn(16 + m)
            for m in ms:
                aggr(16 + m)
            for m in ms:
                flt(16 + m)
            for m in ms:
                ve_pow(16 + m)

        def c_p1(m, h2):
            if h2 == 0:
                cy_t = work.tile([P, H], F32, name="cy_t", tag="w")
                cy[m] = cy_t
            cols = slice(h2 * 512, (h2 + 1) * 512)
            nc.vector.scalar_tensor_tensor(
                out=cy[m][:, cols], in0=halves_of[16 + m][h2], scalar=mv_of[16 + m][:, 0:1], in1=gam4[:, cols],
                op0=ALU.subtract, op1=ALU.mult,
            )

        def c_p2(m, h2):
            cols = slice(h2 * 512, (h2 + 1) * 512)
            nc.vector.scalar_tensor_tensor(
                out=cy[m][:, cols], in0=cy[m][:, cols], scalar=rstd_of[16 + m][:], in1=bet4[:, cols],
                op0=ALU.mult, op1=ALU.add,
            )
            nc.sync.dma_start(out=out_2[m * P : (m + 1) * P, cols], in_=cy[m][:, cols])
            if h2 == 0:
                th_t = nrm.tile([P, H], F32, name="th_t", tag="n")
                th[m] = th_t
            nc.scalar.activation(out=th[m][:, cols], in_=cy[m][:, cols], func=ACT.Tanh)

        def o_back(m):
            back(20 + m, a_tiles[3], m, None, O_BANKS[m])

        hy = {}

        def fin(m, h2):
            if h2 == 0:
                hy_t = work.tile([P, H], F32, name="hy_t", tag="w")
                hy[m] = hy_t
            cols = slice(h2 * 512, (h2 + 1) * 512)
            nc.vector.tensor_tensor(out=hy[m][:, cols], in0=th[m][:, cols], in1=halves_of[20 + m][h2], op=ALU.mult)
            nc.sync.dma_start(out=out_0[m * P : (m + 1) * P, cols], in_=hy[m][:, cols])
            nc.sync.dma_start(out=out_1[m * P : (m + 1) * P, cols], in_=hy[m][:, cols])

        def chain(k):
            bn(k)
            aggr(k)
            flt(k)
            ve_pow(k)

        def close(k):
            nmr(k)
            normalise(k)

        A4 = [0, 1, 2, 3]
        B4 = [4, 5, 6, 7]
        S_BANKS = {0: (0, 1), 1: (2, 3), 2: (0, 1), 3: (2, 3)}
        O_BANKS = {0: (5, 6), 1: (4, 7), 2: (0, 1), 3: (2, 3)}
        T_RING[0] = (5, 6)
        bn(11, (0,))
        quant(12)
        close(10)
        matmuls(12, A4)
        bn(11, (1,))
        for s in (12, 13, 14, 15):
            k = s - 1
            if s > 12:
                matmuls(s, A4)
                if s == 15:
                    s_back(0)
                bn(k, (1,))
            cell_step(k, 10)
            aggr(k)
            cell_step(k, 11)
            flt(k)
            b_step(s)
            matmuls(s, B4)
            cell_step(k, 12)
            ve_pow(k)
            cell_step(k, 13, nc.gpsimd)
            bn(s, (0,))
            close(k)
        ep(3, 0, 0)
        ep(3, 0, 1)
        bn(16)
        cell_step(15, 10)
        aggr(16)
        cell_step(15, 11)
        flt(16)
        c_p1(0, 0)
        ve_pow(16)
        cell_step(15, 13, nc.gpsimd)
        c_p1(0, 1)
        s_back(1)
        ep(3, 0, 2)
        ep(3, 0, 3)
        bn(15, (1,))
        bn(17, (0,))
        cell_step(15, 12)
        s_back(2)
        aggr(15)
        c_p2(0, 0)
        flt(15)
        bn(17, (1,))
        ve_pow(15)
        aggr(17)
        c_p2(0, 1)
        flt(17)
        c_p1(1, 0)
        ve_pow(17)
        c_p1(1, 1)
        close(15)
        o_back(0)
        s_back(3)
        bn(18, (0,))
        fin(0, 0)
        fin(0, 1)
        c_p2(1, 0)
        c_p2(1, 1)
        bn(18, (1,))
        o_back(1)
        ep(3, 1, 0)
        ep(3, 1, 1)
        aggr(18)
        fin(1, 0)
        flt(18)
        c_p1(2, 0)
        ve_pow(18)
        c_p1(2, 1)
        ep(3, 1, 2)
        ep(3, 1, 3)
        fin(1, 1)
        bn(19, (0,))
        c_p2(2, 0)
        bn(19, (1,))
        c_p2(2, 1)
        o_back(2)
        aggr(19)
        fin(2, 0)
        flt(19)
        c_p1(3, 0)
        ve_pow(19)
        c_p1(3, 1)
        fin(2, 1)
        c_p2(3, 0)
        c_p2(3, 1)
        o_back(3)
        fin(3, 0)
        fin(3, 1)
